import numpy as np
import ml_dtypes


def mxq(x, axis, fmt="e4m3"):
    dtype, down = {"e4m3": (ml_dtypes.float8_e4m3fn, 7), "e5m2": (ml_dtypes.float8_e5m2, 14)}[fmt]
    v = np.moveaxis(np.asarray(x, np.float32).astype(ml_dtypes.bfloat16).astype(np.float64), axis, -1)
    blocks = v.reshape(v.shape[:-1] + (-1, 32))
    amax = np.abs(blocks).max(-1, keepdims=True)
    byte = np.maximum(np.where(amax > 0, np.frexp(amax)[1] - 1 + 127, 0) - down, 1)
    scale = np.exp2(byte - 127.0)
    codes = (blocks / scale).astype(np.float32).astype(dtype).astype(np.float64)
    return np.moveaxis((codes * scale).reshape(v.shape), -1, axis)


WIDE = False


def mx_kscale(k):
    if not WIDE:
        return np.ones(k)
    levels = np.array([10, -10, 5, -5, 0])
    a = np.random.permutation(np.resize(levels, k // 512 * 4)).reshape(k // 512, 4)
    idx = np.arange(k)
    return np.exp2(a[idx // 512, idx % 128 // 32])


BF16 = ml_dtypes.bfloat16


def bf(x):
    return np.asarray(x, np.float32).astype(BF16)


def f64(x):
    return np.asarray(x).astype(np.float64)


B, T, D, H, HD = 4, 2048, 512, 2, 64
E = H * HD
HALF = HD // 2


def rotate_half(u):
    return np.concatenate((-u[..., HALF:], u[..., :HALF]), axis=-1)


def setup_inputs():
    s = mx_kscale(D)
    return {"x": bf(np.random.standard_normal((B, T, D)) * s),
            "rope_cos": bf(np.random.random_sample((1, 1, T, HD))),
            "rope_sin": bf(np.random.random_sample((1, 1, T, HD))),
            "qkv_w": bf(np.random.standard_normal((3 * E, D)) / np.sqrt(D) / s[None, :]),
            "qkv_b": bf(np.random.standard_normal(3 * E) * 0.3)}


def reference(x, rope_cos, rope_sin, qkv_w, qkv_b):
    qkv = (mxq(f64(x), 2, "e4m3") @ mxq(f64(qkv_w), 1, "e4m3").T) + f64(qkv_b)
    qkv = qkv.reshape(B, T, 3, H, HD).transpose(2, 0, 3, 1, 4)
    q, k, v = qkv[0], qkv[1], qkv[2]
    cos = f64(rope_cos)[:, :, :T, :]
    sin = f64(rope_sin)[:, :, :T, :]
    q_rot = q * cos + rotate_half(q) * sin
    k_rot = k * cos + rotate_half(k) * sin
    return q_rot, k_rot, v

@@ -1,0 +1,245 @@
+from contextlib import ExitStack
+
+import concourse.mybir as mybir
+from concourse.masks import make_identity
+
+F32 = mybir.dt.float32
+BF16 = mybir.dt.bfloat16
+U32 = mybir.dt.uint32
+U8 = mybir.dt.uint8
+FP8X4 = mybir.dt.float8_e4m3fn_x4
+ALU = mybir.AluOpType
+ACT = mybir.ActivationFunctionType
+
+P = 128
+B, T, D, H, HD = 4, 2048, 512, 2, 64
+HALF = HD // 2
+FLOPS = 2 * B * T * D * 3 * H * HD
+
+JS = 8
+JG = 4
+N_GROUPS = B * T // (P * JG)
+V_EXITS = ()
+
+
+def tile_causalselfattention_pa_t_kernel(
+    tc, x, rope_cos, rope_sin, qkv_w, qkv_b, out_0, out_1, out_2
+):
+    nc = tc.nc
+    outs = [out_0, out_1, out_2]
+    with ExitStack() as ctx:
+        ctx.enter_context(tc.manual_schedule())
+        const = ctx.enter_context(tc.tile_pool(name="const", bufs=1))
+        xin = ctx.enter_context(tc.tile_pool(name="xin", bufs=N_GROUPS))
+        grp = ctx.enter_context(tc.tile_pool(name="grp", bufs=3))
+        cod = ctx.enter_context(tc.tile_pool(name="cod", bufs=3))
+        qbp = ctx.enter_context(tc.tile_pool(name="qbp", bufs=2))
+        mp = ctx.enter_context(tc.tile_pool(name="mp", bufs=4))
+        stp = ctx.enter_context(tc.tile_pool(name="stp", bufs=3))
+        ps_xt = ctx.enter_context(tc.psum_pool(name="ps_xt", bufs=2))
+        ps_acc = ctx.enter_context(tc.psum_pool(name="ps_acc", bufs=3))
+        ps_qk = ctx.enter_context(tc.psum_pool(name="ps_qk", bufs=2))
+        ps_vb = ctx.enter_context(tc.psum_pool(name="ps_vb", bufs=1))
+
+        b_rows = const.tile([P, P], BF16, name="b_rows")
+        nc.vector.memset(b_rows[:], 0.0)
+        ident = const.tile([P, P], F32, name="ident")
+        make_identity(nc, ident[:])
+
+        w_sb = const.tile([P, 3 * D], BF16, name="w_sb")
+        nc.sync.dma_start(
+            out=w_sb[:].rearrange("f (m k) -> f m k", m=3),
+            in_=qkv_w.rearrange("(m f) k -> f m k", m=3),
+        )
+        x_sb = []
+
+        def load_x(g):
+            b, blk, j0 = g // 4, (g // 2) % 2, JG * (g % 2)
+            xt_sb = xin.tile([P, JG * D], BF16, name="x_sb")
+            rows = x[b, blk * P * JS : (blk + 1) * P * JS, :].rearrange("(p j) k -> p j k", j=JS)
+            nc.sync.dma_start(
+                out=xt_sb[:].rearrange("p (j k) -> p j k", j=JG), in_=rows[:, j0 : j0 + JG, :]
+            )
+            x_sb.append(xt_sb)
+
+        load_x(0)
+        nc.sync.dma_start(out=b_rows[0:3, :], in_=qkv_b.rearrange("(m f) -> m f", m=3))
+        cos_sb = const.tile([P, 2, JS, HD], BF16, name="cos_sb")
+        sin_sb = const.tile([P, 2, JS, HD], BF16, name="sin_sb")
+        nc.sync.dma_start(out=cos_sb[:], in_=rope_cos[0, 0].rearrange("(s p j) d -> p s j d", s=2, j=JS))
+        nc.sync.dma_start(out=sin_sb[:], in_=rope_sin[0, 0].rearrange("(s p j) d -> p s j d", s=2, j=JS))
+        for g in range(1, N_GROUPS):
+            load_x(g)
+
+        w_words = w_sb[:].bitcast(F32)
+        w_grouped = const.tile([P, 3 * P * 4], BF16, name="w_grouped", align_bytes=64)
+        wg_words = w_grouped[:].bitcast(F32).rearrange("p (t u) -> p t u", u=2)
+        w_codes = const.tile([P, 3 * P], U32, name="w_codes", align_bytes=64)
+        w_scales = const.tile([P, 3 * P], U8, name="w_scales", align_bytes=64)
+        wt0 = ps_xt.tile([P, 2, 2, P], F32, name="xt")
+        for m in range(2):
+            for u in range(2):
+                c0 = m * 256 + u * P
+                nc.tensor.transpose(wt0[:, m, u, :], w_words[:, c0 : c0 + P], ident[:])
+        nc.vector.tensor_copy(
+            out=wg_words[:, 0 : 2 * P, :].rearrange("p (j t) u -> p j t u", j=2),
+            in_=wt0[:].rearrange("p j u t -> p j t u"),
+        )
+        wt1 = ps_xt.tile([P, 2, 2, P], F32, name="xt")
+        for u in range(2):
+            c0 = 2 * 256 + u * P
+            nc.tensor.transpose(wt1[:, 0, u, :], w_words[:, c0 : c0 + P], ident[:])
+        nc.vector.tensor_copy(
+            out=wg_words[:, 2 * P : 3 * P, :], in_=wt1[:, 0].rearrange("p u t -> p t u")
+        )
+        nc.vector.quantize_mx(
+            out=w_codes[:, 0 : 2 * P].bitcast(FP8X4),
+            scales=w_scales[:, 0 : 2 * P],
+            in_=w_grouped[:, 0 : 2 * P * 4],
+        )
+        nc.vector.quantize_mx(
+            out=w_codes[:, 2 * P : 3 * P].bitcast(FP8X4),
+            scales=w_scales[:, 2 * P : 3 * P],
+            in_=w_grouped[:, 2 * P * 4 : 3 * P * 4],
+        )
+
+        bias_sb = const.tile([P, 4], F32, name="bias_sb")
+        sin_x = const.tile([P, 2, JS, HD], BF16, name="sin_x")
+
+        def small_tables():
+            b_f32 = const.tile([P, P], F32, name="b_f32")
+            nc.vector.tensor_copy(out=b_f32[:], in_=b_rows[:])
+            bt = ps_xt.tile([P, 2, 2, P], F32, name="xt")
+            nc.tensor.transpose(bt[:, 0, 0, :], b_f32[:], ident[:])
+            nc.vector.tensor_copy(out=bias_sb[:, 0:3], in_=bt[:, 0, 0, 0:3])
+            nc.vector.tensor_copy(out=sin_x[:, :, :, 0:HALF], in_=sin_sb[:, :, :, HALF:HD])
+            nc.vector.tensor_scalar_mul(
+                out=sin_x[:, :, :, HALF:HD], in0=sin_sb[:, :, :, 0:HALF], scalar1=-1.0
+            )
+
+        grouped_t = {}
+        codes_t = {}
+        qb_t = {}
+        stg_t = {}
+
+        def stage_a(g):
+            x_words = x_sb[g][:].bitcast(F32)
+            grouped = grp.tile([P, JG * P * 4], BF16, name="grouped", align_bytes=64)
+            g_words = grouped[:].bitcast(F32).rearrange("p (t u) -> p t u", u=2)
+            for pr in range(2):
+                xt = ps_xt.tile([P, 2, 2, P], F32, name="xt")
+                for jj in range(2):
+                    for u in range(2):
+                        c0 = (2 * pr + jj) * 256 + u * P
+                        nc.tensor.transpose(xt[:, jj, u, :], x_words[:, c0 : c0 + P], ident[:])
+                dst = g_words[:, pr * 2 * P : (pr + 1) * 2 * P, :].rearrange(
+                    "p (j t) u -> p j t u", j=2
+                )
+                src = xt[:].rearrange("p j u t -> p j t u")
+                if (g % 4, pr) in V_EXITS:
+                    nc.vector.tensor_copy(out=dst, in_=src)
+                else:
+                    nc.scalar.copy(out=dst, in_=src)
+            grouped_t[g] = grouped
+
+        def stage_b(g):
+            codes = cod.tile([P, JG * P], U32, name="codes", align_bytes=64)
+            scales = cod.tile([P, JG * P], U8, name="scales", align_bytes=64)
+            nc.vector.quantize_mx(
+                out=codes[:].bitcast(FP8X4), scales=scales[:], in_=grouped_t[g][:]
+            )
+            codes_t[g] = (codes, scales)
+
+        def stage_c(g):
+            codes, scales = codes_t[g]
+            accs = []
+            for m in range(3):
+                acc = ps_acc.tile([P, JG * P], F32, name="acc")
+                nc.tensor.matmul_mx(
+                    out=acc[:],
+                    lhsT=w_codes[:, m * P : (m + 1) * P].bitcast(FP8X4),
+                    lhsT_scale=w_scales[:, m * P : (m + 1) * P],
+                    rhs=codes[:].bitcast(FP8X4),
+                    rhs_scale=scales[:],
+                    start=True,
+                    stop=True,
+                )
+                accs.append(acc)
+            qbs = []
+            for m in range(3):
+                qb = qbp.tile([P, JG * P], F32, name="qb%d" % m)
+                nc.scalar.activation(
+                    out=qb[:], in_=accs[m][:], func=ACT.Identity, bias=bias_sb[:, m : m + 1], scale=1.0
+                )
+                qbs.append(qb)
+            qb_t[g] = qbs
+
+        def stage_d(g):
+            b, blk, j0 = g // 4, (g // 2) % 2, JG * (g % 2)
+            qbs = qb_t[g]
+            if g % 2 == 0:
+                stg_new = stp.tile([P, 3, H, JS, HD], F32, name="stg")
+                stg_t[g // 2] = stg_new
+            stg = stg_t[g // 2]
+            qks = []
+            for pr in range(2):
+                qk = ps_qk.tile([P, 2, 2, P], F32, name="qk")
+                for jj in range(2):
+                    for m in range(2):
+                        c0 = (2 * pr + jj) * P
+                        nc.tensor.transpose(qk[:, jj, m, :], qbs[m][:, c0 : c0 + P], ident[:])
+                qks.append(qk)
+            vb = ps_vb.tile([P, JG, P], F32, name="vb")
+            for jj in range(JG):
+                nc.tensor.transpose(vb[:, jj, :], qbs[2][:, jj * P : (jj + 1) * P], ident[:])
+            nc.scalar.copy(
+                out=stg[:, 2, :, j0 : j0 + JG, :].rearrange("p h j d -> p j h d"),
+                in_=vb[:].rearrange("p j (h d) -> p j h d", h=H),
+            )
+            stg_qk = stg[:, 0:2].rearrange("p s h j d -> p j (s h) d")
+            for pr in range(2):
+                jl = j0 + 2 * pr
+                u_ps = qks[pr][:].rearrange("p j m (h d) -> p j (m h) d", h=H)
+                m1 = mp.tile([P, 2, 2 * H, HD], F32, name="m1")
+                m2 = mp.tile([P, 2, 2 * H, HD], F32, name="m2")
+                shape = [P, 2, 2 * H, HD]
+                nc.vector.tensor_tensor(
+                    out=m1[:],
+                    in0=u_ps,
+                    in1=cos_sb[:, blk, jl : jl + 2, :].unsqueeze(2).to_broadcast(shape),
+                    op=ALU.mult,
+                )
+                nc.vector.tensor_tensor(
+                    out=m2[:],
+                    in0=u_ps,
+                    in1=sin_x[:, blk, jl : jl + 2, :].unsqueeze(2).to_broadcast(shape),
+                    op=ALU.mult,
+                )
+                for hf in range(2):
+                    lo, ol = hf * HALF, (1 - hf) * HALF
+                    nc.gpsimd.tensor_tensor(
+                        out=stg_qk[:, jl : jl + 2, :, lo : lo + HALF],
+                        in0=m1[:, :, :, lo : lo + HALF],
+                        in1=m2[:, :, :, ol : ol + HALF],
+                        op=ALU.add,
+                    )
+            if g % 2 == 1:
+                for s in range(3):
+                    nc.sync.dma_start(
+                        out=outs[s][b, :, blk * P * JS : (blk + 1) * P * JS, :].rearrange(
+                            "h (p j) d -> p h (j d)", j=JS
+                        ),
+                        in_=stg[:, s].rearrange("p h j d -> p h (j d)"),
+                    )
+
+        for it in range(-2, N_GROUPS + 1):
+            if 0 <= it - 1:
+                stage_d(it - 1)
+            if 0 <= it < N_GROUPS:
+                stage_c(it)
+            if it + 2 < N_GROUPS:
+                stage_a(it + 2)
+            if 0 <= it + 1 < N_GROUPS:
+                stage_b(it + 1)
+            if it == -1:
+                small_tables()

@@ -19,7 +19,7 @@ FLOPS = 2 * B * T * D * 3 * H * HD
 JS = 8
 JG = 4
 N_GROUPS = B * T // (P * JG)
-V_EXITS = ()
+V_EXITS = ((1, 1), (3, 1))
 
 
 def tile_causalselfattention_pa_t_kernel(
@@ -196,6 +196,16 @@ def tile_causalselfattention_pa_t_kernel(
                 out=stg[:, 2, :, j0 : j0 + JG, :].rearrange("p h j d -> p j h d"),
                 in_=vb[:].rearrange("p j (h d) -> p j h d", h=H),
             )
+            last_block = g // 2 == N_GROUPS // 2 - 1
+
+            def store(s, ja, jn):
+                dram = outs[s][b, :, blk * P * JS : (blk + 1) * P * JS, :].rearrange(
+                    "h (p j) d -> p h j d", j=JS
+                )
+                nc.sync.dma_start(out=dram[:, :, ja : ja + jn, :], in_=stg[:, s, :, ja : ja + jn, :])
+
+            if last_block:
+                store(2, j0, JG)
             stg_qk = stg[:, 0:2].rearrange("p s h j d -> p j (s h) d")
             for pr in range(2):
                 jl = j0 + 2 * pr
@@ -223,14 +233,15 @@ def tile_causalselfattention_pa_t_kernel(
                         in1=m2[:, :, :, ol : ol + HALF],
                         op=ALU.add,
                     )
-            if g % 2 == 1:
+                if g == N_GROUPS - 1:
+                    store(0, jl, 2)
+                    store(1, jl, 2)
+            if g == N_GROUPS - 2:
+                store(0, j0, JG)
+                store(1, j0, JG)
+            if g % 2 == 1 and not last_block:
                 for s in range(3):
-                    nc.sync.dma_start(
-                        out=outs[s][b, :, blk * P * JS : (blk + 1) * P * JS, :].rearrange(
-                            "h (p j) d -> p h (j d)", j=JS
-                        ),
-                        in_=stg[:, s].rearrange("p h j d -> p h (j d)"),
-                    )
+                    store(s, 0, JS)
 
         for it in range(-2, N_GROUPS + 1):
             if 0 <= it - 1:

@@ -19,7 +19,7 @@ FLOPS = 2 * B * T * D * 3 * H * HD
 JS = 8
 JG = 4
 N_GROUPS = B * T // (P * JG)
-V_EXITS = ((1, 1), (3, 1))
+V_EXITS = ()
 
 
 def tile_causalselfattention_pa_t_kernel(
@@ -37,8 +37,8 @@ def tile_causalselfattention_pa_t_kernel(
         mp = ctx.enter_context(tc.tile_pool(name="mp", bufs=4))
         stp = ctx.enter_context(tc.tile_pool(name="stp", bufs=3))
         ps_xt = ctx.enter_context(tc.psum_pool(name="ps_xt", bufs=2))
-        ps_acc = ctx.enter_context(tc.psum_pool(name="ps_acc", bufs=3))
-        ps_qk = ctx.enter_context(tc.psum_pool(name="ps_qk", bufs=2))
+        ps_acc = ctx.enter_context(tc.psum_pool(name="ps_acc", bufs=2))
+        ps_qk = ctx.enter_context(tc.psum_pool(name="ps_qk", bufs=3))
         ps_vb = ctx.enter_context(tc.psum_pool(name="ps_vb", bufs=1))
 
         b_rows = const.tile([P, P], BF16, name="b_rows")
@@ -150,10 +150,10 @@ def tile_causalselfattention_pa_t_kernel(
             )
             codes_t[g] = (codes, scales)
 
-        def stage_c(g):
+        def stage_c(g, ms):
             codes, scales = codes_t[g]
             accs = []
-            for m in range(3):
+            for m in ms:
                 acc = ps_acc.tile([P, JG * P], F32, name="acc")
                 nc.tensor.matmul_mx(
                     out=acc[:],
@@ -165,18 +165,24 @@ def tile_causalselfattention_pa_t_kernel(
                     stop=True,
                 )
                 accs.append(acc)
-            qbs = []
-            for m in range(3):
+            for m, acc in zip(ms, accs):
                 qb = qbp.tile([P, JG * P], F32, name="qb%d" % m)
                 nc.scalar.activation(
-                    out=qb[:], in_=accs[m][:], func=ACT.Identity, bias=bias_sb[:, m : m + 1], scale=1.0
+                    out=qb[:], in_=acc[:], func=ACT.Identity, bias=bias_sb[:, m : m + 1], scale=1.0
                 )
-                qbs.append(qb)
-            qb_t[g] = qbs
+                qb_t[(g, m)] = qb
 
-        def stage_d(g):
-            b, blk, j0 = g // 4, (g // 2) % 2, JG * (g % 2)
-            qbs = qb_t[g]
+        def store(g, s, ja, jn):
+            b, blk = g // 4, (g // 2) % 2
+            dram = outs[s][b, :, blk * P * JS : (blk + 1) * P * JS, :].rearrange(
+                "h (p j) d -> p h j d", j=JS
+            )
+            nc.sync.dma_start(
+                out=dram[:, :, ja : ja + jn, :], in_=stg_t[g // 2][:, s, :, ja : ja + jn, :]
+            )
+
+        def stage_d_qk(g):
+            blk, j0 = (g // 2) % 2, JG * (g % 2)
             if g % 2 == 0:
                 stg_new = stp.tile([P, 3, H, JS, HD], F32, name="stg")
                 stg_t[g // 2] = stg_new
@@ -187,25 +193,8 @@ def tile_causalselfattention_pa_t_kernel(
                 for jj in range(2):
                     for m in range(2):
                         c0 = (2 * pr + jj) * P
-                        nc.tensor.transpose(qk[:, jj, m, :], qbs[m][:, c0 : c0 + P], ident[:])
+                        nc.tensor.transpose(qk[:, jj, m, :], qb_t[(g, m)][:, c0 : c0 + P], ident[:])
                 qks.append(qk)
-            vb = ps_vb.tile([P, JG, P], F32, name="vb")
-            for jj in range(JG):
-                nc.tensor.transpose(vb[:, jj, :], qbs[2][:, jj * P : (jj + 1) * P], ident[:])
-            nc.scalar.copy(
-                out=stg[:, 2, :, j0 : j0 + JG, :].rearrange("p h j d -> p j h d"),
-                in_=vb[:].rearrange("p j (h d) -> p j h d", h=H),
-            )
-            last_block = g // 2 == N_GROUPS // 2 - 1
-
-            def store(s, ja, jn):
-                dram = outs[s][b, :, blk * P * JS : (blk + 1) * P * JS, :].rearrange(
-                    "h (p j) d -> p h j d", j=JS
-                )
-                nc.sync.dma_start(out=dram[:, :, ja : ja + jn, :], in_=stg[:, s, :, ja : ja + jn, :])
-
-            if last_block:
-                store(2, j0, JG)
             stg_qk = stg[:, 0:2].rearrange("p s h j d -> p j (s h) d")
             for pr in range(2):
                 jl = j0 + 2 * pr
@@ -233,23 +222,41 @@ def tile_causalselfattention_pa_t_kernel(
                         in1=m2[:, :, :, ol : ol + HALF],
                         op=ALU.add,
                     )
-                if g == N_GROUPS - 1:
-                    store(0, jl, 2)
-                    store(1, jl, 2)
             if g == N_GROUPS - 2:
-                store(0, j0, JG)
-                store(1, j0, JG)
-            if g % 2 == 1 and not last_block:
+                store(g, 0, j0, JG)
+                store(g, 1, j0, JG)
+
+        def stage_d_v(g):
+            j0 = JG * (g % 2)
+            stg = stg_t[g // 2]
+            vb = ps_vb.tile([P, JG, P], F32, name="vb")
+            for jj in range(JG):
+                nc.tensor.transpose(vb[:, jj, :], qb_t[(g, 2)][:, jj * P : (jj + 1) * P], ident[:])
+            nc.scalar.copy(
+                out=stg[:, 2, :, j0 : j0 + JG, :].rearrange("p h j d -> p j h d"),
+                in_=vb[:].rearrange("p j (h d) -> p j h d", h=H),
+            )
+            if g // 2 == N_GROUPS // 2 - 1:
+                store(g, 2, j0, JG)
+                if g == N_GROUPS - 1:
+                    for jl in (j0, j0 + 2):
+                        store(g, 0, jl, 2)
+                        store(g, 1, jl, 2)
+            elif g % 2 == 1:
                 for s in range(3):
-                    store(s, 0, JS)
+                    store(g, s, 0, JS)
 
         for it in range(-2, N_GROUPS + 1):
             if 0 <= it - 1:
-                stage_d(it - 1)
+                stage_d_qk(it - 1)
             if 0 <= it < N_GROUPS:
-                stage_c(it)
+                stage_c(it, (0, 1))
+            if 0 <= it - 1:
+                stage_d_v(it - 1)
             if it + 2 < N_GROUPS:
                 stage_a(it + 2)
+            if 0 <= it < N_GROUPS:
+                stage_c(it, (2,))
             if 0 <= it + 1 < N_GROUPS:
                 stage_b(it + 1)
             if it == -1:

@@ -34,7 +34,7 @@ def tile_causalselfattention_pa_t_kernel(
         grp = ctx.enter_context(tc.tile_pool(name="grp", bufs=3))
         cod = ctx.enter_context(tc.tile_pool(name="cod", bufs=3))
         qbp = ctx.enter_context(tc.tile_pool(name="qbp", bufs=2))
-        mp = ctx.enter_context(tc.tile_pool(name="mp", bufs=4))
+        mp = ctx.enter_context(tc.tile_pool(name="mp", bufs=3))
         stp = ctx.enter_context(tc.tile_pool(name="stp", bufs=3))
         ps_xt = ctx.enter_context(tc.psum_pool(name="ps_xt", bufs=2))
         ps_acc = ctx.enter_context(tc.psum_pool(name="ps_acc", bufs=2))
@@ -117,6 +117,27 @@ def tile_causalselfattention_pa_t_kernel(
                 out=sin_x[:, :, :, HALF:HD], in0=sin_sb[:, :, :, 0:HALF], scalar1=-1.0
             )
 
+        cs_tab = const.tile([P, 2 * JS // 2, 2, 2 * 2 * H * HD], BF16, name="cs_tab")
+
+        def expand_tables(blk, on_vector):
+            for c, tab in enumerate((cos_sb, sin_x)):
+                for jj in range(2):
+                    dst = cs_tab[:, blk * 4 : (blk + 1) * 4, c, :].rearrange(
+                        "p q (j g d) -> p q j g d", j=2, g=2 * H
+                    )[:, :, jj]
+                    src = (
+                        tab[:, blk]
+                        .rearrange("p (q j) d -> p q j d", j=2)[:, :, jj, :]
+                        .unsqueeze(2)
+                        .to_broadcast([P, 4, 2 * H, HD])
+                    )
+                    if on_vector:
+                        nc.vector.tensor_copy(out=dst, in_=src)
+                    else:
+                        nc.gpsimd.tensor_scalar(
+                            out=dst, in0=src, scalar1=1.0, scalar2=0.0, op0=ALU.mult, op1=ALU.add
+                        )
+
         grouped_t = {}
         codes_t = {}
         qb_t = {}
@@ -195,33 +216,29 @@ def tile_causalselfattention_pa_t_kernel(
                         c0 = (2 * pr + jj) * P
                         nc.tensor.transpose(qk[:, jj, m, :], qb_t[(g, m)][:, c0 : c0 + P], ident[:])
                 qks.append(qk)
-            stg_qk = stg[:, 0:2].rearrange("p s h j d -> p j (s h) d")
+            stg_qk = stg[:, 0:2].rearrange("p s h j d -> p j (s h) d")[:, j0 : j0 + JG].rearrange(
+                "p (r j) g d -> p r j g d", r=2
+            )
+            prod = mp.tile([P, 2, 2, 2 * 2 * H * HD], F32, name="prod")
             for pr in range(2):
-                jl = j0 + 2 * pr
-                u_ps = qks[pr][:].rearrange("p j m (h d) -> p j (m h) d", h=H)
-                m1 = mp.tile([P, 2, 2 * H, HD], F32, name="m1")
-                m2 = mp.tile([P, 2, 2 * H, HD], F32, name="m2")
-                shape = [P, 2, 2 * H, HD]
                 nc.vector.tensor_tensor(
-                    out=m1[:],
-                    in0=u_ps,
-                    in1=cos_sb[:, blk, jl : jl + 2, :].unsqueeze(2).to_broadcast(shape),
+                    out=prod[:, pr],
+                    in0=qks[pr][:]
+                    .rearrange("p j m f -> p (j m f)")
+                    .unsqueeze(1)
+                    .to_broadcast([P, 2, 2 * 2 * H * HD]),
+                    in1=cs_tab[:, blk * 4 + j0 // 2 + pr],
                     op=ALU.mult,
                 )
-                nc.vector.tensor_tensor(
-                    out=m2[:],
-                    in0=u_ps,
-                    in1=sin_x[:, blk, jl : jl + 2, :].unsqueeze(2).to_broadcast(shape),
-                    op=ALU.mult,
+            prod_v = prod[:].rearrange("p r c (j g d) -> p r c j g d", j=2, g=2 * H)
+            for hf in range(2):
+                lo, ol = hf * HALF, (1 - hf) * HALF
+                nc.gpsimd.tensor_tensor(
+                    out=stg_qk[:, :, :, :, lo : lo + HALF],
+                    in0=prod_v[:, :, 0, :, :, lo : lo + HALF],
+                    in1=prod_v[:, :, 1, :, :, ol : ol + HALF],
+                    op=ALU.add,
                 )
-                for hf in range(2):
-                    lo, ol = hf * HALF, (1 - hf) * HALF
-                    nc.gpsimd.tensor_tensor(
-                        out=stg_qk[:, jl : jl + 2, :, lo : lo + HALF],
-                        in0=m1[:, :, :, lo : lo + HALF],
-                        in1=m2[:, :, :, ol : ol + HALF],
-                        op=ALU.add,
-                    )
             if g == N_GROUPS - 2:
                 store(g, 0, j0, JG)
                 store(g, 1, j0, JG)
@@ -239,9 +256,8 @@ def tile_causalselfattention_pa_t_kernel(
             if g // 2 == N_GROUPS // 2 - 1:
                 store(g, 2, j0, JG)
                 if g == N_GROUPS - 1:
-                    for jl in (j0, j0 + 2):
-                        store(g, 0, jl, 2)
-                        store(g, 1, jl, 2)
+                    store(g, 0, j0, JG)
+                    store(g, 1, j0, JG)
             elif g % 2 == 1:
                 for s in range(3):
                     store(g, s, 0, JS)
@@ -261,3 +277,5 @@ def tile_causalselfattention_pa_t_kernel(
                 stage_b(it + 1)
             if it == -1:
                 small_tables()
+                expand_tables(0, True)
+                expand_tables(1, False)

@@ -68,7 +68,10 @@ def tile_causalselfattention_pa_t_kernel(
         sin_sb = const.tile([P, 2, JS, HD], BF16, name="sin_sb")
         nc.sync.dma_start(out=cos_sb[:], in_=rope_cos[0, 0].rearrange("(s p j) d -> p s j d", s=2, j=JS))
         nc.sync.dma_start(out=sin_sb[:], in_=rope_sin[0, 0].rearrange("(s p j) d -> p s j d", s=2, j=JS))
-        for g in range(1, N_GROUPS):
+        load_x(1)
+        bv_bc = const.tile([P, P], BF16, name="bv_bc")
+        nc.sync.dma_start(out=bv_bc[:], in_=qkv_b[2 * P : 3 * P].partition_broadcast(P))
+        for g in range(2, N_GROUPS):
             load_x(g)
 
         w_words = w_sb[:].bitcast(F32)
@@ -243,6 +246,37 @@ def tile_causalselfattention_pa_t_kernel(
                 store(g, 0, j0, JG)
                 store(g, 1, j0, JG)
 
+        vb_t = {}
+
+        def v_direct(g):
+            return g % 2 == 0
+
+        def stage_c_vdirect(g):
+            codes, scales = codes_t[g]
+            vb = ps_vb.tile([P, JG, P], F32, name="vb")
+            for jj in range(JG):
+                nc.tensor.matmul_mx(
+                    out=vb[:, jj, :],
+                    lhsT=codes[:, jj * P : (jj + 1) * P].bitcast(FP8X4),
+                    lhsT_scale=scales[:, jj * P : (jj + 1) * P],
+                    rhs=w_codes[:, 2 * P : 3 * P].bitcast(FP8X4),
+                    rhs_scale=w_scales[:, 2 * P : 3 * P],
+                    start=True,
+                    stop=True,
+                )
+            vb_t[g] = vb
+
+        def stage_d_vdirect(g):
+            j0 = JG * (g % 2)
+            nc.vector.tensor_tensor(
+                out=stg_t[g // 2][:, 2, :, j0 : j0 + JG, :].rearrange("p h j d -> p j h d"),
+                in0=vb_t[g][:].rearrange("p j (h d) -> p j h d", h=H),
+                in1=bv_bc[:].rearrange("p (h d) -> p h d", h=H).unsqueeze(1).to_broadcast([P, JG, H, HD]),
+                op=ALU.add,
+            )
+            if g // 2 == N_GROUPS // 2 - 1:
+                store(g, 2, j0, JG)
+
         def stage_d_v(g):
             j0 = JG * (g % 2)
             stg = stg_t[g // 2]
@@ -265,14 +299,19 @@ def tile_causalselfattention_pa_t_kernel(
         for it in range(-2, N_GROUPS + 1):
             if 0 <= it - 1:
                 stage_d_qk(it - 1)
+                if v_direct(it - 1):
+                    stage_d_vdirect(it - 1)
             if 0 <= it < N_GROUPS:
                 stage_c(it, (0, 1))
-            if 0 <= it - 1:
+            if 0 <= it - 1 and not v_direct(it - 1):
                 stage_d_v(it - 1)
             if it + 2 < N_GROUPS:
                 stage_a(it + 2)
             if 0 <= it < N_GROUPS:
-                stage_c(it, (2,))
+                if v_direct(it):
+                    stage_c_vdirect(it)
+                else:
+                    stage_c(it, (2,))
             if 0 <= it + 1 < N_GROUPS:
                 stage_b(it + 1)
             if it == -1:

@@ -32,8 +32,8 @@ def tile_causalselfattention_pa_t_kernel(
         const = ctx.enter_context(tc.tile_pool(name="const", bufs=1))
         xin = ctx.enter_context(tc.tile_pool(name="xin", bufs=N_GROUPS))
         grp = ctx.enter_context(tc.tile_pool(name="grp", bufs=3))
-        cod = ctx.enter_context(tc.tile_pool(name="cod", bufs=3))
-        qbp = ctx.enter_context(tc.tile_pool(name="qbp", bufs=2))
+        cod = ctx.enter_context(tc.tile_pool(name="cod", bufs=4))
+        qbp = ctx.enter_context(tc.tile_pool(name="qbp", bufs=3))
         mp = ctx.enter_context(tc.tile_pool(name="mp", bufs=3))
         stp = ctx.enter_context(tc.tile_pool(name="stp", bufs=3))
         ps_xt = ctx.enter_context(tc.psum_pool(name="ps_xt", bufs=2))
@@ -68,10 +68,7 @@ def tile_causalselfattention_pa_t_kernel(
         sin_sb = const.tile([P, 2, JS, HD], BF16, name="sin_sb")
         nc.sync.dma_start(out=cos_sb[:], in_=rope_cos[0, 0].rearrange("(s p j) d -> p s j d", s=2, j=JS))
         nc.sync.dma_start(out=sin_sb[:], in_=rope_sin[0, 0].rearrange("(s p j) d -> p s j d", s=2, j=JS))
-        load_x(1)
-        bv_bc = const.tile([P, P], BF16, name="bv_bc")
-        nc.sync.dma_start(out=bv_bc[:], in_=qkv_b[2 * P : 3 * P].partition_broadcast(P))
-        for g in range(2, N_GROUPS):
+        for g in range(1, N_GROUPS):
             load_x(g)
 
         w_words = w_sb[:].bitcast(F32)
@@ -246,37 +243,6 @@ def tile_causalselfattention_pa_t_kernel(
                 store(g, 0, j0, JG)
                 store(g, 1, j0, JG)
 
-        vb_t = {}
-
-        def v_direct(g):
-            return g % 2 == 0
-
-        def stage_c_vdirect(g):
-            codes, scales = codes_t[g]
-            vb = ps_vb.tile([P, JG, P], F32, name="vb")
-            for jj in range(JG):
-                nc.tensor.matmul_mx(
-                    out=vb[:, jj, :],
-                    lhsT=codes[:, jj * P : (jj + 1) * P].bitcast(FP8X4),
-                    lhsT_scale=scales[:, jj * P : (jj + 1) * P],
-                    rhs=w_codes[:, 2 * P : 3 * P].bitcast(FP8X4),
-                    rhs_scale=w_scales[:, 2 * P : 3 * P],
-                    start=True,
-                    stop=True,
-                )
-            vb_t[g] = vb
-
-        def stage_d_vdirect(g):
-            j0 = JG * (g % 2)
-            nc.vector.tensor_tensor(
-                out=stg_t[g // 2][:, 2, :, j0 : j0 + JG, :].rearrange("p h j d -> p j h d"),
-                in0=vb_t[g][:].rearrange("p j (h d) -> p j h d", h=H),
-                in1=bv_bc[:].rearrange("p (h d) -> p h d", h=H).unsqueeze(1).to_broadcast([P, JG, H, HD]),
-                op=ALU.add,
-            )
-            if g // 2 == N_GROUPS // 2 - 1:
-                store(g, 2, j0, JG)
-
         def stage_d_v(g):
             j0 = JG * (g % 2)
             stg = stg_t[g // 2]
@@ -296,25 +262,20 @@ def tile_causalselfattention_pa_t_kernel(
                 for s in range(3):
                     store(g, s, 0, JS)
 
-        for it in range(-2, N_GROUPS + 1):
-            if 0 <= it - 1:
-                stage_d_qk(it - 1)
-                if v_direct(it - 1):
-                    stage_d_vdirect(it - 1)
+        for it in range(-3, N_GROUPS + 2):
+            if 0 <= it - 2:
+                stage_d_qk(it - 2)
             if 0 <= it < N_GROUPS:
                 stage_c(it, (0, 1))
-            if 0 <= it - 1 and not v_direct(it - 1):
-                stage_d_v(it - 1)
-            if it + 2 < N_GROUPS:
-                stage_a(it + 2)
+            if 0 <= it - 2:
+                stage_d_v(it - 2)
+            if it + 3 < N_GROUPS:
+                stage_a(it + 3)
             if 0 <= it < N_GROUPS:
-                if v_direct(it):
-                    stage_c_vdirect(it)
-                else:
-                    stage_c(it, (2,))
-            if 0 <= it + 1 < N_GROUPS:
-                stage_b(it + 1)
-            if it == -1:
+                stage_c(it, (2,))
+            if 0 <= it + 2 < N_GROUPS:
+                stage_b(it + 2)
+            if it == -2:
                 small_tables()
                 expand_tables(0, True)
                 expand_tables(1, False)

@@ -19,7 +19,6 @@ FLOPS = 2 * B * T * D * 3 * H * HD
 JS = 8
 JG = 4
 N_GROUPS = B * T // (P * JG)
-V_EXITS = ()
 
 
 def tile_causalselfattention_pa_t_kernel(
@@ -32,13 +31,13 @@ def tile_causalselfattention_pa_t_kernel(
         const = ctx.enter_context(tc.tile_pool(name="const", bufs=1))
         xin = ctx.enter_context(tc.tile_pool(name="xin", bufs=N_GROUPS))
         grp = ctx.enter_context(tc.tile_pool(name="grp", bufs=3))
-        cod = ctx.enter_context(tc.tile_pool(name="cod", bufs=4))
-        qbp = ctx.enter_context(tc.tile_pool(name="qbp", bufs=3))
-        mp = ctx.enter_context(tc.tile_pool(name="mp", bufs=3))
+        cod = ctx.enter_context(tc.tile_pool(name="cod", bufs=3))
+        qbp = ctx.enter_context(tc.tile_pool(name="qbp", bufs=2))
+        mp = ctx.enter_context(tc.tile_pool(name="mp", bufs=4))
         stp = ctx.enter_context(tc.tile_pool(name="stp", bufs=3))
         ps_xt = ctx.enter_context(tc.psum_pool(name="ps_xt", bufs=2))
-        ps_acc = ctx.enter_context(tc.psum_pool(name="ps_acc", bufs=2))
-        ps_qk = ctx.enter_context(tc.psum_pool(name="ps_qk", bufs=3))
+        ps_acc = ctx.enter_context(tc.psum_pool(name="ps_acc", bufs=3))
+        ps_qk = ctx.enter_context(tc.psum_pool(name="ps_qk", bufs=2))
         ps_vb = ctx.enter_context(tc.psum_pool(name="ps_vb", bufs=1))
 
         b_rows = const.tile([P, P], BF16, name="b_rows")
@@ -117,27 +116,6 @@ def tile_causalselfattention_pa_t_kernel(
                 out=sin_x[:, :, :, HALF:HD], in0=sin_sb[:, :, :, 0:HALF], scalar1=-1.0
             )
 
-        cs_tab = const.tile([P, 2 * JS // 2, 2, 2 * 2 * H * HD], BF16, name="cs_tab")
-
-        def expand_tables(blk, on_vector):
-            for c, tab in enumerate((cos_sb, sin_x)):
-                for jj in range(2):
-                    dst = cs_tab[:, blk * 4 : (blk + 1) * 4, c, :].rearrange(
-                        "p q (j g d) -> p q j g d", j=2, g=2 * H
-                    )[:, :, jj]
-                    src = (
-                        tab[:, blk]
-                        .rearrange("p (q j) d -> p q j d", j=2)[:, :, jj, :]
-                        .unsqueeze(2)
-                        .to_broadcast([P, 4, 2 * H, HD])
-                    )
-                    if on_vector:
-                        nc.vector.tensor_copy(out=dst, in_=src)
-                    else:
-                        nc.gpsimd.tensor_scalar(
-                            out=dst, in0=src, scalar1=1.0, scalar2=0.0, op0=ALU.mult, op1=ALU.add
-                        )
-
         grouped_t = {}
         codes_t = {}
         qb_t = {}
@@ -157,7 +135,7 @@ def tile_causalselfattention_pa_t_kernel(
                     "p (j t) u -> p j t u", j=2
                 )
                 src = xt[:].rearrange("p j u t -> p j t u")
-                if (g % 4, pr) in V_EXITS:
+                if g == 0 and pr == 1:
                     nc.vector.tensor_copy(out=dst, in_=src)
                 else:
                     nc.scalar.copy(out=dst, in_=src)
@@ -171,10 +149,10 @@ def tile_causalselfattention_pa_t_kernel(
             )
             codes_t[g] = (codes, scales)
 
-        def stage_c(g, ms):
+        def stage_c(g):
             codes, scales = codes_t[g]
             accs = []
-            for m in ms:
+            for m in range(3):
                 acc = ps_acc.tile([P, JG * P], F32, name="acc")
                 nc.tensor.matmul_mx(
                     out=acc[:],
@@ -186,24 +164,18 @@ def tile_causalselfattention_pa_t_kernel(
                     stop=True,
                 )
                 accs.append(acc)
-            for m, acc in zip(ms, accs):
+            qbs = []
+            for m in range(3):
                 qb = qbp.tile([P, JG * P], F32, name="qb%d" % m)
                 nc.scalar.activation(
-                    out=qb[:], in_=acc[:], func=ACT.Identity, bias=bias_sb[:, m : m + 1], scale=1.0
+                    out=qb[:], in_=accs[m][:], func=ACT.Identity, bias=bias_sb[:, m : m + 1], scale=1.0
                 )
-                qb_t[(g, m)] = qb
+                qbs.append(qb)
+            qb_t[g] = qbs
 
-        def store(g, s, ja, jn):
-            b, blk = g // 4, (g // 2) % 2
-            dram = outs[s][b, :, blk * P * JS : (blk + 1) * P * JS, :].rearrange(
-                "h (p j) d -> p h j d", j=JS
-            )
-            nc.sync.dma_start(
-                out=dram[:, :, ja : ja + jn, :], in_=stg_t[g // 2][:, s, :, ja : ja + jn, :]
-            )
-
-        def stage_d_qk(g):
-            blk, j0 = (g // 2) % 2, JG * (g % 2)
+        def stage_d(g):
+            b, blk, j0 = g // 4, (g // 2) % 2, JG * (g % 2)
+            qbs = qb_t[g]
             if g % 2 == 0:
                 stg_new = stp.tile([P, 3, H, JS, HD], F32, name="stg")
                 stg_t[g // 2] = stg_new
@@ -214,68 +186,71 @@ def tile_causalselfattention_pa_t_kernel(
                 for jj in range(2):
                     for m in range(2):
                         c0 = (2 * pr + jj) * P
-                        nc.tensor.transpose(qk[:, jj, m, :], qb_t[(g, m)][:, c0 : c0 + P], ident[:])
+                        nc.tensor.transpose(qk[:, jj, m, :], qbs[m][:, c0 : c0 + P], ident[:])
                 qks.append(qk)
-            stg_qk = stg[:, 0:2].rearrange("p s h j d -> p j (s h) d")[:, j0 : j0 + JG].rearrange(
-                "p (r j) g d -> p r j g d", r=2
-            )
-            prod = mp.tile([P, 2, 2, 2 * 2 * H * HD], F32, name="prod")
-            for pr in range(2):
-                nc.vector.tensor_tensor(
-                    out=prod[:, pr],
-                    in0=qks[pr][:]
-                    .rearrange("p j m f -> p (j m f)")
-                    .unsqueeze(1)
-                    .to_broadcast([P, 2, 2 * 2 * H * HD]),
-                    in1=cs_tab[:, blk * 4 + j0 // 2 + pr],
-                    op=ALU.mult,
-                )
-            prod_v = prod[:].rearrange("p r c (j g d) -> p r c j g d", j=2, g=2 * H)
-            for hf in range(2):
-                lo, ol = hf * HALF, (1 - hf) * HALF
-                nc.gpsimd.tensor_tensor(
-                    out=stg_qk[:, :, :, :, lo : lo + HALF],
-                    in0=prod_v[:, :, 0, :, :, lo : lo + HALF],
-                    in1=prod_v[:, :, 1, :, :, ol : ol + HALF],
-                    op=ALU.add,
-                )
-            if g == N_GROUPS - 2:
-                store(g, 0, j0, JG)
-                store(g, 1, j0, JG)
-
-        def stage_d_v(g):
-            j0 = JG * (g % 2)
-            stg = stg_t[g // 2]
             vb = ps_vb.tile([P, JG, P], F32, name="vb")
             for jj in range(JG):
-                nc.tensor.transpose(vb[:, jj, :], qb_t[(g, 2)][:, jj * P : (jj + 1) * P], ident[:])
+                nc.tensor.transpose(vb[:, jj, :], qbs[2][:, jj * P : (jj + 1) * P], ident[:])
             nc.scalar.copy(
                 out=stg[:, 2, :, j0 : j0 + JG, :].rearrange("p h j d -> p j h d"),
                 in_=vb[:].rearrange("p j (h d) -> p j h d", h=H),
             )
-            if g // 2 == N_GROUPS // 2 - 1:
-                store(g, 2, j0, JG)
-                if g == N_GROUPS - 1:
-                    store(g, 0, j0, JG)
-                    store(g, 1, j0, JG)
-            elif g % 2 == 1:
-                for s in range(3):
-                    store(g, s, 0, JS)
+            last_block = g // 2 == N_GROUPS // 2 - 1
 
-        for it in range(-3, N_GROUPS + 2):
-            if 0 <= it - 2:
-                stage_d_qk(it - 2)
+            def store(s, ja, jn):
+                dram = outs[s][b, :, blk * P * JS : (blk + 1) * P * JS, :].rearrange(
+                    "h (p j) d -> p h j d", j=JS
+                )
+                nc.sync.dma_start(out=dram[:, :, ja : ja + jn, :], in_=stg[:, s, :, ja : ja + jn, :])
+
+            if last_block:
+                store(2, j0, JG)
+            stg_qk = stg[:, 0:2].rearrange("p s h j d -> p j (s h) d")
+            for pr in range(2):
+                jl = j0 + 2 * pr
+                u_ps = qks[pr][:].rearrange("p j m (h d) -> p j (m h) d", h=H)
+                m1 = mp.tile([P, 2, 2 * H, HD], F32, name="m1")
+                m2 = mp.tile([P, 2, 2 * H, HD], F32, name="m2")
+                shape = [P, 2, 2 * H, HD]
+                nc.vector.tensor_tensor(
+                    out=m1[:],
+                    in0=u_ps,
+                    in1=cos_sb[:, blk, jl : jl + 2, :].unsqueeze(2).to_broadcast(shape),
+                    op=ALU.mult,
+                )
+                nc.vector.tensor_tensor(
+                    out=m2[:],
+                    in0=u_ps,
+                    in1=sin_x[:, blk, jl : jl + 2, :].unsqueeze(2).to_broadcast(shape),
+                    op=ALU.mult,
+                )
+                for hf in range(2):
+                    lo, ol = hf * HALF, (1 - hf) * HALF
+                    adder = nc.vector if (g == N_GROUPS - 1 and pr == 1) else nc.gpsimd
+                    adder.tensor_tensor(
+                        out=stg_qk[:, jl : jl + 2, :, lo : lo + HALF],
+                        in0=m1[:, :, :, lo : lo + HALF],
+                        in1=m2[:, :, :, ol : ol + HALF],
+                        op=ALU.add,
+                    )
+                if g == N_GROUPS - 1:
+                    store(0, jl, 2)
+                    store(1, jl, 2)
+            if g == N_GROUPS - 2:
+                store(0, j0, JG)
+                store(1, j0, JG)
+            if g % 2 == 1 and not last_block:
+                for s in range(3):
+                    store(s, 0, JS)
+
+        for it in range(-2, N_GROUPS + 1):
+            if 0 <= it - 1:
+                stage_d(it - 1)
             if 0 <= it < N_GROUPS:
-                stage_c(it, (0, 1))
-            if 0 <= it - 2:
-                stage_d_v(it - 2)
-            if it + 3 < N_GROUPS:
-                stage_a(it + 3)
-            if 0 <= it < N_GROUPS:
-                stage_c(it, (2,))
-            if 0 <= it + 2 < N_GROUPS:
-                stage_b(it + 2)
-            if it == -2:
+                stage_c(it)
+            if it + 2 < N_GROUPS:
+                stage_a(it + 2)
+            if 0 <= it + 1 < N_GROUPS:
+                stage_b(it + 1)
+            if it == -1:
                 small_tables()
-                expand_tables(0, True)
-                expand_tables(1, False)

@@ -103,7 +103,8 @@ def tile_causalselfattention_pa_t_kernel(
         )
 
         bias_sb = const.tile([P, 4], F32, name="bias_sb")
-        sin_x = const.tile([P, 2, JS, HD], BF16, name="sin_x")
+        sin_x = const.tile([P, 2, JS, HD], F32, name="sin_x")
+        cos_f = const.tile([P, 2, JS, HD], F32, name="cos_f")
 
         def small_tables():
             b_f32 = const.tile([P, P], F32, name="b_f32")
@@ -111,6 +112,7 @@ def tile_causalselfattention_pa_t_kernel(
             bt = ps_xt.tile([P, 2, 2, P], F32, name="xt")
             nc.tensor.transpose(bt[:, 0, 0, :], b_f32[:], ident[:])
             nc.vector.tensor_copy(out=bias_sb[:, 0:3], in_=bt[:, 0, 0, 0:3])
+            nc.vector.tensor_copy(out=cos_f[:], in_=cos_sb[:])
             nc.vector.tensor_copy(out=sin_x[:, :, :, 0:HALF], in_=sin_sb[:, :, :, HALF:HD])
             nc.vector.tensor_scalar_mul(
                 out=sin_x[:, :, :, HALF:HD], in0=sin_sb[:, :, :, 0:HALF], scalar1=-1.0
@@ -135,10 +137,7 @@ def tile_causalselfattention_pa_t_kernel(
                     "p (j t) u -> p j t u", j=2
                 )
                 src = xt[:].rearrange("p j u t -> p j t u")
-                if g == 0 and pr == 1:
-                    nc.vector.tensor_copy(out=dst, in_=src)
-                else:
-                    nc.scalar.copy(out=dst, in_=src)
+                nc.scalar.copy(out=dst, in_=src)
             grouped_t[g] = grouped
 
         def stage_b(g):
@@ -215,7 +214,7 @@ def tile_causalselfattention_pa_t_kernel(
                 nc.vector.tensor_tensor(
                     out=m1[:],
                     in0=u_ps,
-                    in1=cos_sb[:, blk, jl : jl + 2, :].unsqueeze(2).to_broadcast(shape),
+                    in1=cos_f[:, blk, jl : jl + 2, :].unsqueeze(2).to_broadcast(shape),
                     op=ALU.mult,
                 )
                 nc.vector.tensor_tensor(

from contextlib import ExitStack

import concourse.mybir as mybir
from concourse.masks import make_identity

F32 = mybir.dt.float32
BF16 = mybir.dt.bfloat16
U32 = mybir.dt.uint32
U8 = mybir.dt.uint8
FP8X4 = mybir.dt.float8_e4m3fn_x4
ALU = mybir.AluOpType
ACT = mybir.ActivationFunctionType

P = 128
B, T, D, H, HD = 4, 2048, 512, 2, 64
HALF = HD // 2
FLOPS = 2 * B * T * D * 3 * H * HD

JS = 8
JG = 4
N_GROUPS = B * T // (P * JG)


def tile_causalselfattention_pa_t_kernel(
    tc, x, rope_cos, rope_sin, qkv_w, qkv_b, out_0, out_1, out_2
):
    nc = tc.nc
    outs = [out_0, out_1, out_2]
    with ExitStack() as ctx:
        ctx.enter_context(tc.manual_schedule())
        const = ctx.enter_context(tc.tile_pool(name="const", bufs=1))
        xin = ctx.enter_context(tc.tile_pool(name="xin", bufs=N_GROUPS))
        grp = ctx.enter_context(tc.tile_pool(name="grp", bufs=3))
        cod = ctx.enter_context(tc.tile_pool(name="cod", bufs=3))
        qbp = ctx.enter_context(tc.tile_pool(name="qbp", bufs=2))
        mp = ctx.enter_context(tc.tile_pool(name="mp", bufs=4))
        stp = ctx.enter_context(tc.tile_pool(name="stp", bufs=3))
        ps_xt = ctx.enter_context(tc.psum_pool(name="ps_xt", bufs=2))
        ps_acc = ctx.enter_context(tc.psum_pool(name="ps_acc", bufs=3))
        ps_qk = ctx.enter_context(tc.psum_pool(name="ps_qk", bufs=2))
        ps_vb = ctx.enter_context(tc.psum_pool(name="ps_vb", bufs=1))

        b_rows = const.tile([P, P], BF16, name="b_rows")
        nc.vector.memset(b_rows[:], 0.0)
        ident = const.tile([P, P], F32, name="ident")
        make_identity(nc, ident[:])

        w_sb = const.tile([P, 3 * D], BF16, name="w_sb")
        nc.sync.dma_start(
            out=w_sb[:].rearrange("f (m k) -> f m k", m=3),
            in_=qkv_w.rearrange("(m f) k -> f m k", m=3),
        )
        x_sb = []

        def load_x(g):
            b, blk, j0 = g // 4, (g // 2) % 2, JG * (g % 2)
            xt_sb = xin.tile([P, JG * D], BF16, name="x_sb")
            rows = x[b, blk * P * JS : (blk + 1) * P * JS, :].rearrange("(p j) k -> p j k", j=JS)
            nc.sync.dma_start(
                out=xt_sb[:].rearrange("p (j k) -> p j k", j=JG), in_=rows[:, j0 : j0 + JG, :]
            )
            x_sb.append(xt_sb)

        load_x(0)
        nc.sync.dma_start(out=b_rows[0:3, :], in_=qkv_b.rearrange("(m f) -> m f", m=3))
        cos_sb = const.tile([P, 2, JS, HD], BF16, name="cos_sb")
        sin_sb = const.tile([P, 2, JS, HD], BF16, name="sin_sb")
        nc.sync.dma_start(out=cos_sb[:], in_=rope_cos[0, 0].rearrange("(s p j) d -> p s j d", s=2, j=JS))
        nc.sync.dma_start(out=sin_sb[:], in_=rope_sin[0, 0].rearrange("(s p j) d -> p s j d", s=2, j=JS))
        for g in range(1, N_GROUPS):
            load_x(g)

        w_words = w_sb[:].bitcast(F32)
        w_grouped = const.tile([P, 3 * P * 4], BF16, name="w_grouped", align_bytes=64)
        wg_words = w_grouped[:].bitcast(F32).rearrange("p (t u) -> p t u", u=2)
        w_codes = const.tile([P, 3 * P], U32, name="w_codes", align_bytes=64)
        w_scales = const.tile([P, 3 * P], U8, name="w_scales", align_bytes=64)
        wt0 = ps_xt.tile([P, 2, 2, P], F32, name="xt")
        for m in range(2):
            for u in range(2):
                c0 = m * 256 + u * P
                nc.tensor.transpose(wt0[:, m, u, :], w_words[:, c0 : c0 + P], ident[:])
        nc.vector.tensor_copy(
            out=wg_words[:, 0 : 2 * P, :].rearrange("p (j t) u -> p j t u", j=2),
            in_=wt0[:].rearrange("p j u t -> p j t u"),
        )
        wt1 = ps_xt.tile([P, 2, 2, P], F32, name="xt")
        for u in range(2):
            c0 = 2 * 256 + u * P
            nc.tensor.transpose(wt1[:, 0, u, :], w_words[:, c0 : c0 + P], ident[:])
        nc.vector.tensor_copy(
            out=wg_words[:, 2 * P : 3 * P, :], in_=wt1[:, 0].rearrange("p u t -> p t u")
        )
        nc.vector.quantize_mx(
            out=w_codes[:, 0 : 2 * P].bitcast(FP8X4),
            scales=w_scales[:, 0 : 2 * P],
            in_=w_grouped[:, 0 : 2 * P * 4],
        )
        nc.vector.quantize_mx(
            out=w_codes[:, 2 * P : 3 * P].bitcast(FP8X4),
            scales=w_scales[:, 2 * P : 3 * P],
            in_=w_grouped[:, 2 * P * 4 : 3 * P * 4],
        )

        bias_sb = const.tile([P, 4], F32, name="bias_sb")
        sin_x = const.tile([P, 2, JS, HD], F32, name="sin_x")
        cos_f = const.tile([P, 2, JS, HD], F32, name="cos_f")

        def small_tables():
            b_f32 = const.tile([P, P], F32, name="b_f32")
            nc.vector.tensor_copy(out=b_f32[:], in_=b_rows[:])
            bt = ps_xt.tile([P, 2, 2, P], F32, name="xt")
            nc.tensor.transpose(bt[:, 0, 0, :], b_f32[:], ident[:])
            nc.vector.tensor_copy(out=bias_sb[:, 0:3], in_=bt[:, 0, 0, 0:3])
            nc.vector.tensor_copy(out=cos_f[:], in_=cos_sb[:])
            nc.vector.tensor_copy(out=sin_x[:, :, :, 0:HALF], in_=sin_sb[:, :, :, HALF:HD])
            nc.vector.tensor_scalar_mul(
                out=sin_x[:, :, :, HALF:HD], in0=sin_sb[:, :, :, 0:HALF], scalar1=-1.0
            )

        grouped_t = {}
        codes_t = {}
        qb_t = {}
        stg_t = {}

        def stage_a(g):
            x_words = x_sb[g][:].bitcast(F32)
            grouped = grp.tile([P, JG * P * 4], BF16, name="grouped", align_bytes=64)
            g_words = grouped[:].bitcast(F32).rearrange("p (t u) -> p t u", u=2)
            for pr in range(2):
                xt = ps_xt.tile([P, 2, 2, P], F32, name="xt")
                for jj in range(2):
                    for u in range(2):
                        c0 = (2 * pr + jj) * 256 + u * P
                        nc.tensor.transpose(xt[:, jj, u, :], x_words[:, c0 : c0 + P], ident[:])
                dst = g_words[:, pr * 2 * P : (pr + 1) * 2 * P, :].rearrange(
                    "p (j t) u -> p j t u", j=2
                )
                src = xt[:].rearrange("p j u t -> p j t u")
                nc.scalar.copy(out=dst, in_=src)
            grouped_t[g] = grouped

        def stage_b(g):
            codes = cod.tile([P, JG * P], U32, name="codes", align_bytes=64)
            scales = cod.tile([P, JG * P], U8, name="scales", align_bytes=64)
            nc.vector.quantize_mx(
                out=codes[:].bitcast(FP8X4), scales=scales[:], in_=grouped_t[g][:]
            )
            codes_t[g] = (codes, scales)

        def stage_c(g):
            codes, scales = codes_t[g]
            accs = []
            for m in range(3):
                acc = ps_acc.tile([P, JG * P], F32, name="acc")
                nc.tensor.matmul_mx(
                    out=acc[:],
                    lhsT=w_codes[:, m * P : (m + 1) * P].bitcast(FP8X4),
                    lhsT_scale=w_scales[:, m * P : (m + 1) * P],
                    rhs=codes[:].bitcast(FP8X4),
                    rhs_scale=scales[:],
                    start=True,
                    stop=True,
                )
                accs.append(acc)
            qbs = []
            for m in range(3):
                qb = qbp.tile([P, JG * P], F32, name="qb%d" % m)
                nc.scalar.activation(
                    out=qb[:], in_=accs[m][:], func=ACT.Identity, bias=bias_sb[:, m : m + 1], scale=1.0
                )
                qbs.append(qb)
            qb_t[g] = qbs

        def stage_d(g):
            b, blk, j0 = g // 4, (g // 2) % 2, JG * (g % 2)
            qbs = qb_t[g]
            if g % 2 == 0:
                stg_new = stp.tile([P, 3, H, JS, HD], F32, name="stg")
                stg_t[g // 2] = stg_new
            stg = stg_t[g // 2]
            qks = []
            for pr in range(2):
                qk = ps_qk.tile([P, 2, 2, P], F32, name="qk")
                for jj in range(2):
                    for m in range(2):
                        c0 = (2 * pr + jj) * P
                        nc.tensor.transpose(qk[:, jj, m, :], qbs[m][:, c0 : c0 + P], ident[:])
                qks.append(qk)
            vb = ps_vb.tile([P, JG, P], F32, name="vb")
            for jj in range(JG):
                nc.tensor.transpose(vb[:, jj, :], qbs[2][:, jj * P : (jj + 1) * P], ident[:])
            nc.scalar.copy(
                out=stg[:, 2, :, j0 : j0 + JG, :].rearrange("p h j d -> p j h d"),
                in_=vb[:].rearrange("p j (h d) -> p j h d", h=H),
            )
            last_block = g // 2 == N_GROUPS // 2 - 1

            def store(s, ja, jn):
                dram = outs[s][b, :, blk * P * JS : (blk + 1) * P * JS, :].rearrange(
                    "h (p j) d -> p h j d", j=JS
                )
                nc.sync.dma_start(out=dram[:, :, ja : ja + jn, :], in_=stg[:, s, :, ja : ja + jn, :])

            if last_block:
                store(2, j0, JG)
            stg_qk = stg[:, 0:2].rearrange("p s h j d -> p j (s h) d")
            for pr in range(2):
                jl = j0 + 2 * pr
                u_ps = qks[pr][:].rearrange("p j m (h d) -> p j (m h) d", h=H)
                m1 = mp.tile([P, 2, 2 * H, HD], F32, name="m1")
                m2 = mp.tile([P, 2, 2 * H, HD], F32, name="m2")
                shape = [P, 2, 2 * H, HD]
                nc.vector.tensor_tensor(
                    out=m1[:],
                    in0=u_ps,
                    in1=cos_f[:, blk, jl : jl + 2, :].unsqueeze(2).to_broadcast(shape),
                    op=ALU.mult,
                )
                nc.vector.tensor_tensor(
                    out=m2[:],
                    in0=u_ps,
                    in1=sin_x[:, blk, jl : jl + 2, :].unsqueeze(2).to_broadcast(shape),
                    op=ALU.mult,
                )
                for hf in range(2):
                    lo, ol = hf * HALF, (1 - hf) * HALF
                    adder = nc.vector if (g == N_GROUPS - 1 and pr == 1) else nc.gpsimd
                    adder.tensor_tensor(
                        out=stg_qk[:, jl : jl + 2, :, lo : lo + HALF],
                        in0=m1[:, :, :, lo : lo + HALF],
                        in1=m2[:, :, :, ol : ol + HALF],
                        op=ALU.add,
                    )
                if g == N_GROUPS - 1:
                    store(0, jl, 2)
                    store(1, jl, 2)
            if g == N_GROUPS - 2:
                store(0, j0, JG)
                store(1, j0, JG)
            if g % 2 == 1 and not last_block:
                for s in range(3):
                    store(s, 0, JS)

        for it in range(-2, N_GROUPS + 1):
            if 0 <= it - 1:
                stage_d(it - 1)
            if 0 <= it < N_GROUPS:
                stage_c(it)
            if it + 2 < N_GROUPS:
                stage_a(it + 2)
            if 0 <= it + 1 < N_GROUPS:
                stage_b(it + 1)
            if it == -1:
                small_tables()
